import numpy as np
import ml_dtypes


def mxq(x, axis, fmt="e4m3"):
    dtype, down = {"e4m3": (ml_dtypes.float8_e4m3fn, 7), "e5m2": (ml_dtypes.float8_e5m2, 14)}[fmt]
    v = np.moveaxis(np.asarray(x, np.float32).astype(ml_dtypes.bfloat16).astype(np.float64), axis, -1)
    blocks = v.reshape(v.shape[:-1] + (-1, 32))
    amax = np.abs(blocks).max(-1, keepdims=True)
    byte = np.maximum(np.where(amax > 0, np.frexp(amax)[1] - 1 + 127, 0) - down, 1)
    scale = np.exp2(byte - 127.0)
    codes = (blocks / scale).astype(np.float32).astype(dtype).astype(np.float64)
    return np.moveaxis((codes * scale).reshape(v.shape), -1, axis)


WIDE = False


def mx_kscale(k):
    if not WIDE:
        return np.ones(k)
    levels = np.array([10, -10, 5, -5, 0])
    a = np.random.permutation(np.resize(levels, k // 512 * 4)).reshape(k // 512, 4)
    idx = np.arange(k)
    return np.exp2(a[idx // 512, idx % 128 // 32])


BF16 = ml_dtypes.bfloat16


def bf(x):
    return np.asarray(x, np.float32).astype(BF16)


def f64(x):
    return np.asarray(x).astype(np.float64)


B, T, D, S, R = 2, 512, 2048, 8, 64
EPS = float(np.finfo(np.float32).eps)


def silu(v):
    return v / (1.0 + np.exp(-v))


def sigmoid(v):
    return 1.0 / (1.0 + np.exp(-v))


def setup_inputs():
    g = 0.5 + 1.5 * np.random.random((B, T, 1))
    g[:, ::4] *= 2.0 ** -12
    s = mx_kscale(D)
    c = 2.0 ** np.round(np.log2(np.sqrt(np.mean(s * s))))
    return {"h": bf(np.random.standard_normal((B, T, D)) * g * s / c),
            "w_down": bf(np.random.standard_normal((S, R, D)) * 1.5 / np.sqrt(D) * c / s),
            "w_up": bf(np.random.standard_normal((S, D, R)) * S / np.sqrt(S * R)),
            "gate_bias": bf(0.8 + 0.1 * np.random.standard_normal(1))}


def reference(h, w_down, w_up, gate_bias):
    h64 = f64(h)
    rms = np.sqrt(np.mean(h64 * h64, axis=-1, keepdims=True) + EPS)
    h_norm = h64 / rms
    a = mxq(h_norm, 2, "e4m3") @ mxq(f64(w_down).reshape(S * R, D), 1, "e4m3").T
    view = silu(a)
    upd = mxq(view, 2, "e4m3") @ mxq(f64(w_up).transpose(0, 2, 1).reshape(S * R, D), 0, "e4m3")
    mean_update = upd / S
    gate = sigmoid(f64(gate_bias))
    return h64 + gate * mean_update

@@ -1,0 +1,242 @@
+from contextlib import ExitStack
+
+import concourse.mybir as mybir
+from concourse.masks import make_identity
+
+F32 = mybir.dt.float32
+BF16 = mybir.dt.bfloat16
+U32 = mybir.dt.uint32
+U8 = mybir.dt.uint8
+FP8X4 = mybir.dt.float8_e4m3fn_x4
+ACT = mybir.ActivationFunctionType
+ALU = mybir.AluOpType
+
+P = 128
+PACK = 4
+K_PASS = P * PACK
+TOKENS = 2 * 512
+D = 2048
+SPOKES = 8
+RANK = 64
+SR = SPOKES * RANK
+BLOCKS = TOKENS // P
+PASSES = D // K_PASS
+D_WORDS = D // 2
+BANK = 512
+PER_BANK = BANK // P
+D_PER_PART = D // P
+EPS = 2.0 ** -23
+
+FLOPS = 2 * TOKENS * D * SR * 2
+
+
+def transpose_bank(nc, psum, words, first_word, ident):
+    bank = psum.tile([P, PER_BANK, P], F32, tag="transposed")
+    for j in range(PER_BANK):
+        nc.tensor.transpose(bank[:, j, :], words[:, first_word + j * P : first_word + (j + 1) * P], ident[:])
+    return bank
+
+
+def tile_spokelayer_kernel(tc, h, w_down, w_up, gate_bias, out):
+    nc = tc.nc
+    h_rows = h.flatten_outer_dims()
+    out_rows = out.flatten_outer_dims()
+    wd_rows = w_down.flatten_outer_dims()
+
+    with ExitStack() as ctx:
+        keep = ctx.enter_context(tc.tile_pool(name="keep", bufs=1))
+        work = ctx.enter_context(tc.tile_pool(name="work", bufs=4))
+        results = ctx.enter_context(tc.tile_pool(name="results", bufs=4))
+        psum_t = ctx.enter_context(tc.psum_pool(name="psum_t", bufs=3))
+        psum_a = ctx.enter_context(tc.psum_pool(name="psum_a", bufs=2))
+        psum_o = ctx.enter_context(tc.psum_pool(name="psum_o", bufs=3))
+
+        h_all = keep.tile([P, BLOCKS, D], BF16)
+        wd_sb = keep.tile([P, PACK * D], BF16)
+        wu_sb = keep.tile([P, SPOKES * D_PER_PART * RANK], BF16)
+        gate_raw = keep.tile([P, 1], BF16)
+
+        def load_h(b):
+            nc.sync.dma_start(out=h_all[:, b, :], in_=h_rows[b * P : (b + 1) * P, :])
+
+        nc.scalar.dma_start(out=gate_raw[:], in_=gate_bias.partition_broadcast(P))
+
+        def load_w_down(t):
+            u, e = divmod(t, 2)
+            nc.sync.dma_start(
+                out=wd_sb[:, t * D : (t + 1) * D],
+                in_=wd_rows[u * 2 * P : (u + 1) * 2 * P, :].rearrange("(p e) d -> p e d", e=2)[:, e, :],
+            )
+
+        load_w_down(0)
+        load_h(0)
+        load_w_down(1)
+        load_h(1)
+        load_w_down(2)
+        load_w_down(3)
+        load_h(2)
+        half = SPOKES // 2
+        row = D_PER_PART * RANK
+        for s0 in (0, half):
+            nc.sync.dma_start(
+                out=wu_sb[:, s0 * row : (s0 + half) * row].rearrange("p (s x) -> p s x", s=half),
+                in_=w_up[s0 : s0 + half].rearrange("s (p j) r -> p s (j r)", j=D_PER_PART),
+            )
+        for b in range(3, BLOCKS):
+            load_h(b)
+
+        ident = keep.tile([P, P], F32)
+        make_identity(nc, ident[:])
+        neg_half = keep.tile([P, 1], F32)
+        nc.gpsimd.memset(neg_half[:], -0.5)
+        table_warmer = keep.tile([P, 1], F32)
+        nc.scalar.activation(out=table_warmer[:], in_=neg_half[:], func=ACT.Silu)
+        gate_tanh = keep.tile([P, 1], F32)
+        nc.scalar.activation(out=gate_tanh[:], in_=gate_raw[:], func=ACT.Tanh, scale=0.5)
+        gate_eighth = keep.tile([P, 1], F32)
+        nc.vector.tensor_scalar(
+            out=gate_eighth[:],
+            in0=gate_tanh[:],
+            scalar1=0.5 / SPOKES,
+            scalar2=0.5 / SPOKES,
+            op0=ALU.mult,
+            op1=ALU.add,
+        )
+
+        wd_words = wd_sb[:].bitcast(F32)
+        wd_grp = keep.tile([P, PACK * D], BF16, align_bytes=64)
+        wd_grp_words = wd_grp[:].bitcast(F32).rearrange("p (c n u) -> p c n u", n=P, u=2)
+        wd_codes = keep.tile([P, PACK * PASSES * P], U32, align_bytes=64)
+        wd_scales = keep.tile([P, PACK * PASSES * P], U8, align_bytes=64)
+        for t in range(PACK):
+            for pair in range(PASSES // 2):
+                bank = transpose_bank(nc, psum_t, wd_words, t * D_WORDS + pair * BANK, ident)
+                c = t * PASSES + 2 * pair
+                nc.vector.tensor_copy(
+                    out=wd_grp_words[:, c : c + 2, :, :],
+                    in_=bank[:].rearrange("p (g u) n -> p g n u", u=2),
+                )
+            nc.vector.quantize_mx(
+                out=wd_codes[:, t * BANK : (t + 1) * BANK].bitcast(FP8X4),
+                scales=wd_scales[:, t * BANK : (t + 1) * BANK],
+                in_=wd_grp[:, t * D : (t + 1) * D],
+            )
+
+        wu_by_d = keep.tile([P, D_PER_PART * SR], BF16)
+        wu_grp = keep.tile([P, PACK * D], BF16, align_bytes=64)
+        wu_grp_words = wu_grp[:].bitcast(F32).rearrange("c (p j u) -> c p j u", j=D_PER_PART, u=2)
+        wu_codes = keep.tile([P, D], U32, align_bytes=64)
+        wu_scales = keep.tile([P, D], U8, align_bytes=64)
+
+        def prepare_w_up():
+            wu_words = wu_by_d[:].bitcast(F32)
+            for j0 in range(0, D_PER_PART, PACK):
+                nc.vector.tensor_copy(
+                    out=wu_by_d[:, j0 * SR : (j0 + PACK) * SR].rearrange("p (j s r) -> p j s r", s=SPOKES, r=RANK),
+                    in_=wu_sb[:].rearrange("p (s j r) -> p j s r", s=SPOKES, r=RANK)[:, j0 : j0 + PACK],
+                )
+                for pair in range(j0 // 2, j0 // 2 + PACK // 2):
+                    bank = transpose_bank(nc, psum_t, wu_words, pair * BANK, ident)
+                    nc.scalar.copy(
+                        out=wu_grp_words[:, :, 2 * pair : 2 * pair + 2, :],
+                        in_=bank[:].rearrange("c (j u) p -> c p j u", u=2),
+                    )
+            for q in range(2):
+                nc.vector.quantize_mx(
+                    out=wu_codes[:, q * 2 * BANK : (q + 1) * 2 * BANK].bitcast(FP8X4),
+                    scales=wu_scales[:, q * 2 * BANK : (q + 1) * 2 * BANK],
+                    in_=wu_grp[:, q * 2 * D : (q + 1) * 2 * D],
+                )
+
+        sum_sq = keep.tile([P, BLOCKS], F32)
+        mean_sq = keep.tile([P, BLOCKS], F32)
+        inv_rms = keep.tile([P, BLOCKS], F32)
+        view_codes = keep.tile([P, BLOCKS * P], U32, align_bytes=64)
+        view_scales = keep.tile([P, BLOCKS * P], U8, align_bytes=64)
+
+        def down(b):
+            one = slice(b, b + 1)
+            squares = work.tile([P, D], BF16)
+            nc.scalar.activation(out=squares[:], in_=h_all[:, b, :], func=ACT.Square, accum_out=sum_sq[:, one])
+            nc.gpsimd.tensor_scalar(
+                out=mean_sq[:, one], in0=sum_sq[:, one], scalar1=1.0 / D, scalar2=EPS, op0=ALU.mult, op1=ALU.add
+            )
+            nc.gpsimd.tensor_tensor(out=inv_rms[:, one], in0=mean_sq[:, one], in1=neg_half[:], op=ALU.pow)
+            h_norm = work.tile([P, D], BF16)
+            nc.vector.tensor_scalar(
+                out=h_norm[:], in0=h_all[:, b, :], scalar1=inv_rms[:, one], scalar2=None, op0=ALU.mult
+            )
+            h_grp = work.tile([P, D], BF16, align_bytes=64)
+            h_grp_words = h_grp[:].bitcast(F32).rearrange("p (g n u) -> p g n u", n=P, u=2)
+            for pair in range(PASSES // 2):
+                bank = transpose_bank(nc, psum_t, h_norm[:].bitcast(F32), pair * BANK, ident)
+                nc.scalar.copy(
+                    out=h_grp_words[:, 2 * pair : 2 * pair + 2, :, :],
+                    in_=bank[:].rearrange("p (g u) n -> p g n u", u=2),
+                )
+            h_codes = work.tile([P, PASSES * P], U32, align_bytes=64)
+            h_scales = work.tile([P, PASSES * P], U8, align_bytes=64)
+            nc.vector.quantize_mx(out=h_codes[:].bitcast(FP8X4), scales=h_scales[:], in_=h_grp[:])
+
+            a_ps = psum_a.tile([P, PACK, P], F32)
+            for t in range(PACK):
+                for g in range(PASSES):
+                    w_cols = slice((t * PASSES + g) * P, (t * PASSES + g + 1) * P)
+                    x_cols = slice(g * P, (g + 1) * P)
+                    nc.tensor.matmul_mx(
+                        out=a_ps[:, t, :],
+                        lhsT=wd_codes[:, w_cols].bitcast(FP8X4),
+                        lhsT_scale=wd_scales[:, w_cols],
+                        rhs=h_codes[:, x_cols].bitcast(FP8X4),
+                        rhs_scale=h_scales[:, x_cols],
+                        start=(g == 0),
+                        stop=(g == PASSES - 1),
+                    )
+            view_grp = work.tile([P, PACK * P], BF16, align_bytes=64)
+            nc.scalar.activation(
+                out=view_grp[:].rearrange("p (n t) -> p n t", t=PACK),
+                in_=a_ps[:].rearrange("p t n -> p n t"),
+                func=ACT.Silu,
+            )
+            cols = slice(b * P, (b + 1) * P)
+            nc.vector.quantize_mx(
+                out=view_codes[:, cols].bitcast(FP8X4), scales=view_scales[:, cols], in_=view_grp[:]
+            )
+
+        def up(b):
+            cols = slice(b * P, (b + 1) * P)
+            for c in range(D // BANK):
+                d_cols = slice(c * BANK, (c + 1) * BANK)
+                if c % 2 == 0:
+                    out_sb = results.tile([P, 2 * BANK], F32)
+                upd = psum_o.tile([P, BANK], F32)
+                nc.tensor.matmul_mx(
+                    out=upd[:],
+                    lhsT=view_codes[:, cols].bitcast(FP8X4),
+                    lhsT_scale=view_scales[:, cols],
+                    rhs=wu_codes[:, d_cols].bitcast(FP8X4),
+                    rhs_scale=wu_scales[:, d_cols],
+                    start=True,
+                    stop=True,
+                )
+                nc.vector.scalar_tensor_tensor(
+                    out=out_sb[:, (c % 2) * BANK : (c % 2 + 1) * BANK],
+                    in0=upd[:],
+                    scalar=gate_eighth[:, 0:1],
+                    in1=h_all[:, b, d_cols],
+                    op0=ALU.mult,
+                    op1=ALU.add,
+                )
+                if c % 2 == 1:
+                    nc.sync.dma_start(
+                        out=out_rows[b * P : (b + 1) * P, (c - 1) * BANK : (c + 1) * BANK], in_=out_sb[:]
+                    )
+
+        down(0)
+        down(1)
+        prepare_w_up()
+        for b in range(2, BLOCKS):
+            down(b)
+            up(b - 2)
+        up(BLOCKS - 2)
+        up(BLOCKS - 1)

@@ -24,16 +24,21 @@ PASSES = D // K_PASS
 D_WORDS = D // 2
 BANK = 512
 PER_BANK = BANK // P
-D_PER_PART = D // P
+HALVES = 2
+D_HALF = D // HALVES
+ROWS = D_HALF // P
+HALF_BANKS = ROWS * 2 // PER_BANK
 EPS = 2.0 ** -23
 
 FLOPS = 2 * TOKENS * D * SR * 2
 
 
-def transpose_bank(nc, psum, words, first_word, ident):
-    bank = psum.tile([P, PER_BANK, P], F32, tag="transposed")
-    for j in range(PER_BANK):
-        nc.tensor.transpose(bank[:, j, :], words[:, first_word + j * P : first_word + (j + 1) * P], ident[:])
+def transpose_bank(nc, pool, tag, words, first_word, ident):
+    bank = pool.tile([P, BANK], F32, tag=tag)
+    for i in range(PER_BANK):
+        nc.tensor.transpose(
+            bank[:, i * P : (i + 1) * P], words[:, first_word + i * P : first_word + (i + 1) * P], ident[:]
+        )
     return bank
 
 
@@ -45,21 +50,28 @@ def tile_spokelayer_kernel(tc, h, w_down, w_up, gate_bias, out):
 
     with ExitStack() as ctx:
         keep = ctx.enter_context(tc.tile_pool(name="keep", bufs=1))
-        work = ctx.enter_context(tc.tile_pool(name="work", bufs=4))
+        work = ctx.enter_context(tc.tile_pool(name="work", bufs=3))
         results = ctx.enter_context(tc.tile_pool(name="results", bufs=4))
-        psum_t = ctx.enter_context(tc.psum_pool(name="psum_t", bufs=3))
-        psum_a = ctx.enter_context(tc.psum_pool(name="psum_a", bufs=2))
-        psum_o = ctx.enter_context(tc.psum_pool(name="psum_o", bufs=3))
+        psum_h = ctx.enter_context(tc.psum_pool(name="psum_h", bufs=3))
+        psum_a = ctx.enter_context(tc.psum_pool(name="psum_a", bufs=1))
+        psum_o = ctx.enter_context(tc.psum_pool(name="psum_o", bufs=4))
+        ctx.enter_context(tc.manual_schedule())
+
+        ident = keep.tile([P, P], F32)
+        make_identity(nc, ident[:])
+        neg_half = keep.tile([P, 1], F32)
+        nc.gpsimd.memset(neg_half[:], -0.5)
+        table_warmer = keep.tile([P, 1], F32)
+        nc.scalar.activation(out=table_warmer[:], in_=neg_half[:], func=ACT.Silu)
 
         h_all = keep.tile([P, BLOCKS, D], BF16)
         wd_sb = keep.tile([P, PACK * D], BF16)
-        wu_sb = keep.tile([P, SPOKES * D_PER_PART * RANK], BF16)
+        wu_sb = keep.tile([P, HALVES * SPOKES * ROWS * RANK], BF16)
         gate_raw = keep.tile([P, 1], BF16)
+        wu_half = SPOKES * ROWS * RANK
 
         def load_h(b):
             nc.sync.dma_start(out=h_all[:, b, :], in_=h_rows[b * P : (b + 1) * P, :])
-
-        nc.scalar.dma_start(out=gate_raw[:], in_=gate_bias.partition_broadcast(P))
 
         def load_w_down(t):
             u, e = divmod(t, 2)
@@ -68,32 +80,28 @@ def tile_spokelayer_kernel(tc, h, w_down, w_up, gate_bias, out):
                 in_=wd_rows[u * 2 * P : (u + 1) * 2 * P, :].rearrange("(p e) d -> p e d", e=2)[:, e, :],
             )
 
-        load_w_down(0)
+        def load_w_up(half):
+            nc.sync.dma_start(
+                out=wu_sb[:, half * wu_half : (half + 1) * wu_half].rearrange("p (s x) -> p s x", s=SPOKES),
+                in_=w_up[:, half * D_HALF : (half + 1) * D_HALF, :].rearrange("s (p j) r -> p s (j r)", j=ROWS),
+            )
+
+        nc.sync.dma_start(out=gate_raw[:], in_=gate_bias.partition_broadcast(P))
         load_h(0)
+        load_w_down(0)
         load_w_down(1)
         load_h(1)
         load_w_down(2)
         load_w_down(3)
         load_h(2)
-        half = SPOKES // 2
-        row = D_PER_PART * RANK
-        for s0 in (0, half):
-            nc.sync.dma_start(
-                out=wu_sb[:, s0 * row : (s0 + half) * row].rearrange("p (s x) -> p s x", s=half),
-                in_=w_up[s0 : s0 + half].rearrange("s (p j) r -> p s (j r)", j=D_PER_PART),
-            )
+        load_w_up(0)
+        load_w_up(1)
         for b in range(3, BLOCKS):
             load_h(b)
 
-        ident = keep.tile([P, P], F32)
-        make_identity(nc, ident[:])
-        neg_half = keep.tile([P, 1], F32)
-        nc.gpsimd.memset(neg_half[:], -0.5)
-        table_warmer = keep.tile([P, 1], F32)
-        nc.scalar.activation(out=table_warmer[:], in_=neg_half[:], func=ACT.Silu)
         gate_tanh = keep.tile([P, 1], F32)
-        nc.scalar.activation(out=gate_tanh[:], in_=gate_raw[:], func=ACT.Tanh, scale=0.5)
         gate_eighth = keep.tile([P, 1], F32)
+        nc.scalar.activation(out=gate_tanh[:], in_=gate_raw[:], func=ACT.Tanh, scale=0.5)
         nc.vector.tensor_scalar(
             out=gate_eighth[:],
             in0=gate_tanh[:],
@@ -103,50 +111,84 @@ def tile_spokelayer_kernel(tc, h, w_down, w_up, gate_bias, out):
             op1=ALU.add,
         )
 
+        tiles = {}
+
         wd_words = wd_sb[:].bitcast(F32)
         wd_grp = keep.tile([P, PACK * D], BF16, align_bytes=64)
         wd_grp_words = wd_grp[:].bitcast(F32).rearrange("p (c n u) -> p c n u", n=P, u=2)
         wd_codes = keep.tile([P, PACK * PASSES * P], U32, align_bytes=64)
         wd_scales = keep.tile([P, PACK * PASSES * P], U8, align_bytes=64)
-        for t in range(PACK):
+
+        def group_w_down(t):
+            if not 0 <= t < PACK:
+                return
             for pair in range(PASSES // 2):
-                bank = transpose_bank(nc, psum_t, wd_words, t * D_WORDS + pair * BANK, ident)
+                bank = transpose_bank(nc, psum_o, "wide", wd_words, t * D_WORDS + pair * BANK, ident)
                 c = t * PASSES + 2 * pair
-                nc.vector.tensor_copy(
-                    out=wd_grp_words[:, c : c + 2, :, :],
-                    in_=bank[:].rearrange("p (g u) n -> p g n u", u=2),
-                )
+                copy = nc.vector.tensor_copy if pair == 0 else nc.scalar.copy
+                copy(out=wd_grp_words[:, c : c + 2, :, :], in_=bank[:].rearrange("p (g u n) -> p g n u", g=2, u=2))
+
+        def quantise_w_down(t):
+            if not 0 <= t < PACK:
+                return
             nc.vector.quantize_mx(
                 out=wd_codes[:, t * BANK : (t + 1) * BANK].bitcast(FP8X4),
                 scales=wd_scales[:, t * BANK : (t + 1) * BANK],
                 in_=wd_grp[:, t * D : (t + 1) * D],
             )
 
-        wu_by_d = keep.tile([P, D_PER_PART * SR], BF16)
+        wu_by_d = keep.tile([P, HALVES * ROWS * SR], BF16)
+        wu_words = wu_by_d[:].bitcast(F32)
         wu_grp = keep.tile([P, PACK * D], BF16, align_bytes=64)
-        wu_grp_words = wu_grp[:].bitcast(F32).rearrange("c (p j u) -> c p j u", j=D_PER_PART, u=2)
+        wu_grp_words = wu_grp[:].bitcast(F32).rearrange("c (x p j u) -> c x p j u", x=HALVES, j=ROWS, u=2)
         wu_codes = keep.tile([P, D], U32, align_bytes=64)
         wu_scales = keep.tile([P, D], U8, align_bytes=64)
 
-        def prepare_w_up():
-            wu_words = wu_by_d[:].bitcast(F32)
-            for j0 in range(0, D_PER_PART, PACK):
+        def regroup_w_up(half):
+            if not 0 <= half < HALVES:
+                return
+            loaded = wu_sb[:, half * wu_half : (half + 1) * wu_half].rearrange(
+                "p (s j r) -> p j s r", s=SPOKES, r=RANK
+            )
+            for j0 in range(0, ROWS, PACK):
+                first = (half * ROWS + j0) * SR
                 nc.vector.tensor_copy(
-                    out=wu_by_d[:, j0 * SR : (j0 + PACK) * SR].rearrange("p (j s r) -> p j s r", s=SPOKES, r=RANK),
-                    in_=wu_sb[:].rearrange("p (s j r) -> p j s r", s=SPOKES, r=RANK)[:, j0 : j0 + PACK],
+                    out=wu_by_d[:, first : first + PACK * SR].rearrange("p (j s r) -> p j s r", s=SPOKES, r=RANK),
+                    in_=loaded[:, j0 : j0 + PACK],
                 )
-                for pair in range(j0 // 2, j0 // 2 + PACK // 2):
-                    bank = transpose_bank(nc, psum_t, wu_words, pair * BANK, ident)
-                    nc.scalar.copy(
-                        out=wu_grp_words[:, :, 2 * pair : 2 * pair + 2, :],
-                        in_=bank[:].rearrange("c (j u) p -> c p j u", u=2),
-                    )
-            for q in range(2):
-                nc.vector.quantize_mx(
-                    out=wu_codes[:, q * 2 * BANK : (q + 1) * 2 * BANK].bitcast(FP8X4),
-                    scales=wu_scales[:, q * 2 * BANK : (q + 1) * 2 * BANK],
-                    in_=wu_grp[:, q * 2 * D : (q + 1) * 2 * D],
+
+        def transpose_w_up(half):
+            if not 0 <= half < HALVES:
+                return
+            for i in range(HALF_BANKS):
+                tiles["wu_bank", half, i] = transpose_bank(
+                    nc, psum_o, "wide", wu_words, (half * HALF_BANKS + i) * BANK, ident
                 )
+
+        def group_w_up(half):
+            if not 0 <= half < HALVES:
+                return
+            for i in range(HALF_BANKS):
+                copy = nc.scalar.copy if i < HALF_BANKS // 2 else nc.vector.tensor_copy
+                copy(
+                    out=wu_grp_words[:, half, :, 2 * i : 2 * i + 2, :],
+                    in_=tiles["wu_bank", half, i][:].rearrange("c (j u p) -> c p j u", j=2, u=2),
+                )
+
+        def quantise_w_up(half):
+            if not 0 <= half < HALVES:
+                return
+            nc.vector.quantize_mx(
+                out=wu_codes[:, half * D_HALF : (half + 1) * D_HALF].bitcast(FP8X4),
+                scales=wu_scales[:, half * D_HALF : (half + 1) * D_HALF],
+                in_=wu_grp[:, half * PACK * D_HALF : (half + 1) * PACK * D_HALF],
+            )
+
+        def w_up_turn(k):
+            quantise_w_up(k - 2)
+            regroup_w_up(k)
+            group_w_up(k - 1)
+            transpose_w_up(k)
 
         sum_sq = keep.tile([P, BLOCKS], F32)
         mean_sq = keep.tile([P, BLOCKS], F32)
@@ -154,7 +196,12 @@ def tile_spokelayer_kernel(tc, h, w_down, w_up, gate_bias, out):
         view_codes = keep.tile([P, BLOCKS * P], U32, align_bytes=64)
         view_scales = keep.tile([P, BLOCKS * P], U8, align_bytes=64)
 
-        def down(b):
+        def exists(b):
+            return 0 <= b < BLOCKS
+
+        def square_sum(b):
+            if not exists(b):
+                return
             one = slice(b, b + 1)
             squares = work.tile([P, D], BF16)
             nc.scalar.activation(out=squares[:], in_=h_all[:, b, :], func=ACT.Square, accum_out=sum_sq[:, one])
@@ -162,22 +209,48 @@ def tile_spokelayer_kernel(tc, h, w_down, w_up, gate_bias, out):
                 out=mean_sq[:, one], in0=sum_sq[:, one], scalar1=1.0 / D, scalar2=EPS, op0=ALU.mult, op1=ALU.add
             )
             nc.gpsimd.tensor_tensor(out=inv_rms[:, one], in0=mean_sq[:, one], in1=neg_half[:], op=ALU.pow)
+
+        def normalise(b):
+            if not exists(b):
+                return
             h_norm = work.tile([P, D], BF16)
             nc.vector.tensor_scalar(
-                out=h_norm[:], in0=h_all[:, b, :], scalar1=inv_rms[:, one], scalar2=None, op0=ALU.mult
+                out=h_norm[:], in0=h_all[:, b, :], scalar1=inv_rms[:, b : b + 1], scalar2=None, op0=ALU.mult
             )
+            tiles["h_norm", b] = h_norm
+
+        def transpose_h(b):
+            if not exists(b):
+                return
+            for pair in range(PASSES // 2):
+                tiles["h_bank", b, pair] = transpose_bank(
+                    nc, psum_h, "narrow", tiles["h_norm", b][:].bitcast(F32), pair * BANK, ident
+                )
+
+        def group_h(b):
+            if not exists(b):
+                return
             h_grp = work.tile([P, D], BF16, align_bytes=64)
             h_grp_words = h_grp[:].bitcast(F32).rearrange("p (g n u) -> p g n u", n=P, u=2)
             for pair in range(PASSES // 2):
-                bank = transpose_bank(nc, psum_t, h_norm[:].bitcast(F32), pair * BANK, ident)
                 nc.scalar.copy(
                     out=h_grp_words[:, 2 * pair : 2 * pair + 2, :, :],
-                    in_=bank[:].rearrange("p (g u) n -> p g n u", u=2),
+                    in_=tiles["h_bank", b, pair][:].rearrange("p (g u n) -> p g n u", g=2, u=2),
                 )
+            tiles["h_grp", b] = h_grp
+
+        def quantise_h(b):
+            if not exists(b):
+                return
             h_codes = work.tile([P, PASSES * P], U32, align_bytes=64)
             h_scales = work.tile([P, PASSES * P], U8, align_bytes=64)
-            nc.vector.quantize_mx(out=h_codes[:].bitcast(FP8X4), scales=h_scales[:], in_=h_grp[:])
+            nc.vector.quantize_mx(out=h_codes[:].bitcast(FP8X4), scales=h_scales[:], in_=tiles["h_grp", b][:])
+            tiles["h_codes", b] = h_codes
+            tiles["h_scales", b] = h_scales
 
+        def down(b):
+            if not exists(b):
+                return
             a_ps = psum_a.tile([P, PACK, P], F32)
             for t in range(PACK):
                 for g in range(PASSES):
@@ -187,29 +260,39 @@ def tile_spokelayer_kernel(tc, h, w_down, w_up, gate_bias, out):
                         out=a_ps[:, t, :],
                         lhsT=wd_codes[:, w_cols].bitcast(FP8X4),
                         lhsT_scale=wd_scales[:, w_cols],
-                        rhs=h_codes[:, x_cols].bitcast(FP8X4),
-                        rhs_scale=h_scales[:, x_cols],
+                        rhs=tiles["h_codes", b][:, x_cols].bitcast(FP8X4),
+                        rhs_scale=tiles["h_scales", b][:, x_cols],
                         start=(g == 0),
                         stop=(g == PASSES - 1),
                     )
+            tiles["a", b] = a_ps
+
+        def silu(b):
+            if not exists(b):
+                return
             view_grp = work.tile([P, PACK * P], BF16, align_bytes=64)
             nc.scalar.activation(
                 out=view_grp[:].rearrange("p (n t) -> p n t", t=PACK),
-                in_=a_ps[:].rearrange("p t n -> p n t"),
+                in_=tiles["a", b][:].rearrange("p t n -> p n t"),
                 func=ACT.Silu,
             )
+            tiles["view_grp", b] = view_grp
+
+        def quantise_view(b):
+            if not exists(b):
+                return
             cols = slice(b * P, (b + 1) * P)
             nc.vector.quantize_mx(
-                out=view_codes[:, cols].bitcast(FP8X4), scales=view_scales[:, cols], in_=view_grp[:]
+                out=view_codes[:, cols].bitcast(FP8X4), scales=view_scales[:, cols], in_=tiles["view_grp", b][:]
             )
 
         def up(b):
+            if not exists(b):
+                return
             cols = slice(b * P, (b + 1) * P)
             for c in range(D // BANK):
                 d_cols = slice(c * BANK, (c + 1) * BANK)
-                if c % 2 == 0:
-                    out_sb = results.tile([P, 2 * BANK], F32)
-                upd = psum_o.tile([P, BANK], F32)
+                upd = psum_o.tile([P, BANK], F32, tag="wide")
                 nc.tensor.matmul_mx(
                     out=upd[:],
                     lhsT=view_codes[:, cols].bitcast(FP8X4),
@@ -219,24 +302,40 @@ def tile_spokelayer_kernel(tc, h, w_down, w_up, gate_bias, out):
                     start=True,
                     stop=True,
                 )
-                nc.vector.scalar_tensor_tensor(
-                    out=out_sb[:, (c % 2) * BANK : (c % 2 + 1) * BANK],
-                    in0=upd[:],
-                    scalar=gate_eighth[:, 0:1],
-                    in1=h_all[:, b, d_cols],
-                    op0=ALU.mult,
-                    op1=ALU.add,
-                )
-                if c % 2 == 1:
-                    nc.sync.dma_start(
-                        out=out_rows[b * P : (b + 1) * P, (c - 1) * BANK : (c + 1) * BANK], in_=out_sb[:]
-                    )
+                tiles["upd", b, c] = upd
 
-        down(0)
-        down(1)
-        prepare_w_up()
-        for b in range(2, BLOCKS):
-            down(b)
-            up(b - 2)
-        up(BLOCKS - 2)
-        up(BLOCKS - 1)
+        def finish(b):
+            if not exists(b):
+                return
+            for side in range(2):
+                out_sb = results.tile([P, 2 * BANK], F32)
+                for i in range(2):
+                    c = 2 * side + i
+                    nc.vector.scalar_tensor_tensor(
+                        out=out_sb[:, i * BANK : (i + 1) * BANK],
+                        in0=tiles["upd", b, c][:],
+                        scalar=gate_eighth[:, 0:1],
+                        in1=h_all[:, b, c * BANK : (c + 1) * BANK],
+                        op0=ALU.mult,
+                        op1=ALU.add,
+                    )
+                nc.sync.dma_start(
+                    out=out_rows[b * P : (b + 1) * P, side * 2 * BANK : (side + 1) * 2 * BANK], in_=out_sb[:]
+                )
+
+        for n in range(-1, BLOCKS + 3):
+            square_sum(n + 1)
+            normalise(n)
+            transpose_h(n)
+            for t in (2 * n + 2, 2 * n + 3):
+                group_w_down(t)
+                quantise_w_down(t - 1)
+            quantise_h(n - 1)
+            down(n - 1)
+            w_up_turn(2 * n - 2)
+            group_h(n)
+            quantise_view(n - 2)
+            finish(n - 3)
+            w_up_turn(2 * n - 1)
+            up(n - 2)
+            silu(n - 1)

@@ -326,10 +326,10 @@ def tile_spokelayer_kernel(tc, h, w_down, w_up, gate_bias, out):
         for n in range(-1, BLOCKS + 3):
             square_sum(n + 1)
             normalise(n)
-            transpose_h(n)
             for t in (2 * n + 2, 2 * n + 3):
                 group_w_down(t)
                 quantise_w_down(t - 1)
+            transpose_h(n)
             quantise_h(n - 1)
             down(n - 1)
             w_up_turn(2 * n - 2)

@@ -51,7 +51,7 @@ def tile_spokelayer_kernel(tc, h, w_down, w_up, gate_bias, out):
     with ExitStack() as ctx:
         keep = ctx.enter_context(tc.tile_pool(name="keep", bufs=1))
         work = ctx.enter_context(tc.tile_pool(name="work", bufs=3))
-        results = ctx.enter_context(tc.tile_pool(name="results", bufs=4))
+        results = ctx.enter_context(tc.tile_pool(name="results", bufs=8))
         psum_h = ctx.enter_context(tc.psum_pool(name="psum_h", bufs=3))
         psum_a = ctx.enter_context(tc.psum_pool(name="psum_a", bufs=1))
         psum_o = ctx.enter_context(tc.psum_pool(name="psum_o", bufs=4))
@@ -307,21 +307,18 @@ def tile_spokelayer_kernel(tc, h, w_down, w_up, gate_bias, out):
         def finish(b):
             if not exists(b):
                 return
-            for side in range(2):
-                out_sb = results.tile([P, 2 * BANK], F32)
-                for i in range(2):
-                    c = 2 * side + i
-                    nc.vector.scalar_tensor_tensor(
-                        out=out_sb[:, i * BANK : (i + 1) * BANK],
-                        in0=tiles["upd", b, c][:],
-                        scalar=gate_eighth[:, 0:1],
-                        in1=h_all[:, b, c * BANK : (c + 1) * BANK],
-                        op0=ALU.mult,
-                        op1=ALU.add,
-                    )
-                nc.sync.dma_start(
-                    out=out_rows[b * P : (b + 1) * P, side * 2 * BANK : (side + 1) * 2 * BANK], in_=out_sb[:]
+            for c in range(D // BANK):
+                d_cols = slice(c * BANK, (c + 1) * BANK)
+                out_sb = results.tile([P, BANK], F32)
+                nc.vector.scalar_tensor_tensor(
+                    out=out_sb[:],
+                    in0=tiles["upd", b, c][:],
+                    scalar=gate_eighth[:, 0:1],
+                    in1=h_all[:, b, d_cols],
+                    op0=ALU.mult,
+                    op1=ALU.add,
                 )
+                nc.sync.dma_start(out=out_rows[b * P : (b + 1) * P, d_cols], in_=out_sb[:])
 
         for n in range(-1, BLOCKS + 3):
             square_sum(n + 1)

@@ -28,7 +28,7 @@ HALVES = 2
 D_HALF = D // HALVES
 ROWS = D_HALF // P
 HALF_BANKS = ROWS * 2 // PER_BANK
-EPS = 2.0 ** -23
+PAD = 128
 
 FLOPS = 2 * TOKENS * D * SR * 2
 
@@ -64,14 +64,15 @@ def tile_spokelayer_kernel(tc, h, w_down, w_up, gate_bias, out):
         table_warmer = keep.tile([P, 1], F32)
         nc.scalar.activation(out=table_warmer[:], in_=neg_half[:], func=ACT.Silu)
 
-        h_all = keep.tile([P, BLOCKS, D], BF16)
+        h_all = keep.tile([P, BLOCKS, D + PAD], BF16)
+        nc.gpsimd.memset(h_all[:, :, D : D + 1], 2.0 ** -6)
         wd_sb = keep.tile([P, PACK * D], BF16)
         wu_sb = keep.tile([P, HALVES * SPOKES * ROWS * RANK], BF16)
         gate_raw = keep.tile([P, 1], BF16)
         wu_half = SPOKES * ROWS * RANK
 
         def load_h(b):
-            nc.sync.dma_start(out=h_all[:, b, :], in_=h_rows[b * P : (b + 1) * P, :])
+            nc.sync.dma_start(out=h_all[:, b, :D], in_=h_rows[b * P : (b + 1) * P, :])
 
         def load_w_down(t):
             u, e = divmod(t, 2)
@@ -86,7 +87,6 @@ def tile_spokelayer_kernel(tc, h, w_down, w_up, gate_bias, out):
                 in_=w_up[:, half * D_HALF : (half + 1) * D_HALF, :].rearrange("s (p j) r -> p s (j r)", j=ROWS),
             )
 
-        nc.sync.dma_start(out=gate_raw[:], in_=gate_bias.partition_broadcast(P))
         load_h(0)
         load_w_down(0)
         load_w_down(1)
@@ -98,18 +98,23 @@ def tile_spokelayer_kernel(tc, h, w_down, w_up, gate_bias, out):
         load_w_up(1)
         for b in range(3, BLOCKS):
             load_h(b)
+            if b == 4:
+                nc.sync.dma_start(out=gate_raw[:], in_=gate_bias.partition_broadcast(P))
 
         gate_tanh = keep.tile([P, 1], F32)
         gate_eighth = keep.tile([P, 1], F32)
-        nc.scalar.activation(out=gate_tanh[:], in_=gate_raw[:], func=ACT.Tanh, scale=0.5)
-        nc.vector.tensor_scalar(
-            out=gate_eighth[:],
-            in0=gate_tanh[:],
-            scalar1=0.5 / SPOKES,
-            scalar2=0.5 / SPOKES,
-            op0=ALU.mult,
-            op1=ALU.add,
-        )
+        def gate_on_scalar():
+            nc.scalar.activation(out=gate_tanh[:], in_=gate_raw[:], func=ACT.Tanh, scale=0.5)
+
+        def gate_on_vector():
+            nc.vector.tensor_scalar(
+                out=gate_eighth[:],
+                in0=gate_tanh[:],
+                scalar1=0.5 / SPOKES,
+                scalar2=0.5 / SPOKES,
+                op0=ALU.mult,
+                op1=ALU.add,
+            )
 
         tiles = {}
 
@@ -169,7 +174,7 @@ def tile_spokelayer_kernel(tc, h, w_down, w_up, gate_bias, out):
             if not 0 <= half < HALVES:
                 return
             for i in range(HALF_BANKS):
-                copy = nc.scalar.copy if i < HALF_BANKS // 2 else nc.vector.tensor_copy
+                copy = nc.vector.tensor_copy if half == 0 else nc.scalar.copy
                 copy(
                     out=wu_grp_words[:, half, :, 2 * i : 2 * i + 2, :],
                     in_=tiles["wu_bank", half, i][:].rearrange("c (j u p) -> c p j u", j=2, u=2),
@@ -190,7 +195,6 @@ def tile_spokelayer_kernel(tc, h, w_down, w_up, gate_bias, out):
             group_w_up(k - 1)
             transpose_w_up(k)
 
-        sum_sq = keep.tile([P, BLOCKS], F32)
         mean_sq = keep.tile([P, BLOCKS], F32)
         inv_rms = keep.tile([P, BLOCKS], F32)
         view_codes = keep.tile([P, BLOCKS * P], U32, align_bytes=64)
@@ -203,10 +207,9 @@ def tile_spokelayer_kernel(tc, h, w_down, w_up, gate_bias, out):
             if not exists(b):
                 return
             one = slice(b, b + 1)
-            squares = work.tile([P, D], BF16)
-            nc.scalar.activation(out=squares[:], in_=h_all[:, b, :], func=ACT.Square, accum_out=sum_sq[:, one])
-            nc.gpsimd.tensor_scalar(
-                out=mean_sq[:, one], in0=sum_sq[:, one], scalar1=1.0 / D, scalar2=EPS, op0=ALU.mult, op1=ALU.add
+            squares = work.tile([P, D + 1], BF16)
+            nc.scalar.activation(
+                out=squares[:], in_=h_all[:, b, : D + 1], func=ACT.Square, scale=D ** -0.5, accum_out=mean_sq[:, one]
             )
             nc.gpsimd.tensor_tensor(out=inv_rms[:, one], in0=mean_sq[:, one], in1=neg_half[:], op=ALU.pow)
 
@@ -215,7 +218,7 @@ def tile_spokelayer_kernel(tc, h, w_down, w_up, gate_bias, out):
                 return
             h_norm = work.tile([P, D], BF16)
             nc.vector.tensor_scalar(
-                out=h_norm[:], in0=h_all[:, b, :], scalar1=inv_rms[:, b : b + 1], scalar2=None, op0=ALU.mult
+                out=h_norm[:], in0=h_all[:, b, :D], scalar1=inv_rms[:, b : b + 1], scalar2=None, op0=ALU.mult
             )
             tiles["h_norm", b] = h_norm
 
@@ -331,8 +334,12 @@ def tile_spokelayer_kernel(tc, h, w_down, w_up, gate_bias, out):
             down(n - 1)
             w_up_turn(2 * n - 2)
             group_h(n)
+            if n == 2:
+                gate_on_scalar()
             quantise_view(n - 2)
             finish(n - 3)
             w_up_turn(2 * n - 1)
             up(n - 2)
             silu(n - 1)
+            if n == 2:
+                gate_on_vector()

from contextlib import ExitStack

import concourse.mybir as mybir
from concourse.masks import make_identity

F32 = mybir.dt.float32
BF16 = mybir.dt.bfloat16
U32 = mybir.dt.uint32
U8 = mybir.dt.uint8
FP8X4 = mybir.dt.float8_e4m3fn_x4
ACT = mybir.ActivationFunctionType
ALU = mybir.AluOpType

P = 128
PACK = 4
K_PASS = P * PACK
TOKENS = 2 * 512
D = 2048
SPOKES = 8
RANK = 64
SR = SPOKES * RANK
BLOCKS = TOKENS // P
PASSES = D // K_PASS
D_WORDS = D // 2
BANK = 512
PER_BANK = BANK // P
HALVES = 2
D_HALF = D // HALVES
ROWS = D_HALF // P
HALF_BANKS = ROWS * 2 // PER_BANK
PAD = 128

FLOPS = 2 * TOKENS * D * SR * 2


def transpose_bank(nc, pool, tag, words, first_word, ident):
    bank = pool.tile([P, BANK], F32, tag=tag)
    for i in range(PER_BANK):
        nc.tensor.transpose(
            bank[:, i * P : (i + 1) * P], words[:, first_word + i * P : first_word + (i + 1) * P], ident[:]
        )
    return bank


def tile_spokelayer_kernel(tc, h, w_down, w_up, gate_bias, out):
    nc = tc.nc
    h_rows = h.flatten_outer_dims()
    out_rows = out.flatten_outer_dims()
    wd_rows = w_down.flatten_outer_dims()

    with ExitStack() as ctx:
        keep = ctx.enter_context(tc.tile_pool(name="keep", bufs=1))
        work = ctx.enter_context(tc.tile_pool(name="work", bufs=3))
        results = ctx.enter_context(tc.tile_pool(name="results", bufs=8))
        psum_h = ctx.enter_context(tc.psum_pool(name="psum_h", bufs=3))
        psum_a = ctx.enter_context(tc.psum_pool(name="psum_a", bufs=1))
        psum_o = ctx.enter_context(tc.psum_pool(name="psum_o", bufs=4))
        ctx.enter_context(tc.manual_schedule())

        ident = keep.tile([P, P], F32)
        make_identity(nc, ident[:])
        neg_half = keep.tile([P, 1], F32)
        nc.gpsimd.memset(neg_half[:], -0.5)
        table_warmer = keep.tile([P, 1], F32)
        nc.scalar.activation(out=table_warmer[:], in_=neg_half[:], func=ACT.Silu)

        h_all = keep.tile([P, BLOCKS, D + PAD], BF16)
        nc.gpsimd.memset(h_all[:, :, D : D + 1], 2.0 ** -6)
        wd_sb = keep.tile([P, PACK * D], BF16)
        wu_sb = keep.tile([P, HALVES * SPOKES * ROWS * RANK], BF16)
        gate_raw = keep.tile([P, 1], BF16)
        wu_half = SPOKES * ROWS * RANK

        def load_h(b):
            nc.sync.dma_start(out=h_all[:, b, :D], in_=h_rows[b * P : (b + 1) * P, :])

        def load_w_down(t):
            u, e = divmod(t, 2)
            nc.sync.dma_start(
                out=wd_sb[:, t * D : (t + 1) * D],
                in_=wd_rows[u * 2 * P : (u + 1) * 2 * P, :].rearrange("(p e) d -> p e d", e=2)[:, e, :],
            )

        def load_w_up(half):
            nc.sync.dma_start(
                out=wu_sb[:, half * wu_half : (half + 1) * wu_half].rearrange("p (s x) -> p s x", s=SPOKES),
                in_=w_up[:, half * D_HALF : (half + 1) * D_HALF, :].rearrange("s (p j) r -> p s (j r)", j=ROWS),
            )

        load_h(0)
        load_w_down(0)
        load_w_down(1)
        load_h(1)
        load_w_down(2)
        load_w_down(3)
        load_h(2)
        load_w_up(0)
        load_w_up(1)
        for b in range(3, BLOCKS):
            load_h(b)
            if b == 4:
                nc.sync.dma_start(out=gate_raw[:], in_=gate_bias.partition_broadcast(P))

        gate_tanh = keep.tile([P, 1], F32)
        gate_eighth = keep.tile([P, 1], F32)
        def gate_on_scalar():
            nc.scalar.activation(out=gate_tanh[:], in_=gate_raw[:], func=ACT.Tanh, scale=0.5)

        def gate_on_vector():
            nc.vector.tensor_scalar(
                out=gate_eighth[:],
                in0=gate_tanh[:],
                scalar1=0.5 / SPOKES,
                scalar2=0.5 / SPOKES,
                op0=ALU.mult,
                op1=ALU.add,
            )

        tiles = {}

        wd_words = wd_sb[:].bitcast(F32)
        wd_grp = keep.tile([P, PACK * D], BF16, align_bytes=64)
        wd_grp_words = wd_grp[:].bitcast(F32).rearrange("p (c n u) -> p c n u", n=P, u=2)
        wd_codes = keep.tile([P, PACK * PASSES * P], U32, align_bytes=64)
        wd_scales = keep.tile([P, PACK * PASSES * P], U8, align_bytes=64)

        def group_w_down(t):
            if not 0 <= t < PACK:
                return
            for pair in range(PASSES // 2):
                bank = transpose_bank(nc, psum_o, "wide", wd_words, t * D_WORDS + pair * BANK, ident)
                c = t * PASSES + 2 * pair
                copy = nc.vector.tensor_copy if pair == 0 else nc.scalar.copy
                copy(out=wd_grp_words[:, c : c + 2, :, :], in_=bank[:].rearrange("p (g u n) -> p g n u", g=2, u=2))

        def quantise_w_down(t):
            if not 0 <= t < PACK:
                return
            nc.vector.quantize_mx(
                out=wd_codes[:, t * BANK : (t + 1) * BANK].bitcast(FP8X4),
                scales=wd_scales[:, t * BANK : (t + 1) * BANK],
                in_=wd_grp[:, t * D : (t + 1) * D],
            )

        wu_by_d = keep.tile([P, HALVES * ROWS * SR], BF16)
        wu_words = wu_by_d[:].bitcast(F32)
        wu_grp = keep.tile([P, PACK * D], BF16, align_bytes=64)
        wu_grp_words = wu_grp[:].bitcast(F32).rearrange("c (x p j u) -> c x p j u", x=HALVES, j=ROWS, u=2)
        wu_codes = keep.tile([P, D], U32, align_bytes=64)
        wu_scales = keep.tile([P, D], U8, align_bytes=64)

        def regroup_w_up(half):
            if not 0 <= half < HALVES:
                return
            loaded = wu_sb[:, half * wu_half : (half + 1) * wu_half].rearrange(
                "p (s j r) -> p j s r", s=SPOKES, r=RANK
            )
            for j0 in range(0, ROWS, PACK):
                first = (half * ROWS + j0) * SR
                nc.vector.tensor_copy(
                    out=wu_by_d[:, first : first + PACK * SR].rearrange("p (j s r) -> p j s r", s=SPOKES, r=RANK),
                    in_=loaded[:, j0 : j0 + PACK],
                )

        def transpose_w_up(half):
            if not 0 <= half < HALVES:
                return
            for i in range(HALF_BANKS):
                tiles["wu_bank", half, i] = transpose_bank(
                    nc, psum_o, "wide", wu_words, (half * HALF_BANKS + i) * BANK, ident
                )

        def group_w_up(half):
            if not 0 <= half < HALVES:
                return
            for i in range(HALF_BANKS):
                copy = nc.vector.tensor_copy if half == 0 else nc.scalar.copy
                copy(
                    out=wu_grp_words[:, half, :, 2 * i : 2 * i + 2, :],
                    in_=tiles["wu_bank", half, i][:].rearrange("c (j u p) -> c p j u", j=2, u=2),
                )

        def quantise_w_up(half):
            if not 0 <= half < HALVES:
                return
            nc.vector.quantize_mx(
                out=wu_codes[:, half * D_HALF : (half + 1) * D_HALF].bitcast(FP8X4),
                scales=wu_scales[:, half * D_HALF : (half + 1) * D_HALF],
                in_=wu_grp[:, half * PACK * D_HALF : (half + 1) * PACK * D_HALF],
            )

        def w_up_turn(k):
            quantise_w_up(k - 2)
            regroup_w_up(k)
            group_w_up(k - 1)
            transpose_w_up(k)

        mean_sq = keep.tile([P, BLOCKS], F32)
        inv_rms = keep.tile([P, BLOCKS], F32)
        view_codes = keep.tile([P, BLOCKS * P], U32, align_bytes=64)
        view_scales = keep.tile([P, BLOCKS * P], U8, align_bytes=64)

        def exists(b):
            return 0 <= b < BLOCKS

        def square_sum(b):
            if not exists(b):
                return
            one = slice(b, b + 1)
            squares = work.tile([P, D + 1], BF16)
            nc.scalar.activation(
                out=squares[:], in_=h_all[:, b, : D + 1], func=ACT.Square, scale=D ** -0.5, accum_out=mean_sq[:, one]
            )
            nc.gpsimd.tensor_tensor(out=inv_rms[:, one], in0=mean_sq[:, one], in1=neg_half[:], op=ALU.pow)

        def normalise(b):
            if not exists(b):
                return
            h_norm = work.tile([P, D], BF16)
            nc.vector.tensor_scalar(
                out=h_norm[:], in0=h_all[:, b, :D], scalar1=inv_rms[:, b : b + 1], scalar2=None, op0=ALU.mult
            )
            tiles["h_norm", b] = h_norm

        def transpose_h(b):
            if not exists(b):
                return
            for pair in range(PASSES // 2):
                tiles["h_bank", b, pair] = transpose_bank(
                    nc, psum_h, "narrow", tiles["h_norm", b][:].bitcast(F32), pair * BANK, ident
                )

        def group_h(b):
            if not exists(b):
                return
            h_grp = work.tile([P, D], BF16, align_bytes=64)
            h_grp_words = h_grp[:].bitcast(F32).rearrange("p (g n u) -> p g n u", n=P, u=2)
            for pair in range(PASSES // 2):
                nc.scalar.copy(
                    out=h_grp_words[:, 2 * pair : 2 * pair + 2, :, :],
                    in_=tiles["h_bank", b, pair][:].rearrange("p (g u n) -> p g n u", g=2, u=2),
                )
            tiles["h_grp", b] = h_grp

        def quantise_h(b):
            if not exists(b):
                return
            h_codes = work.tile([P, PASSES * P], U32, align_bytes=64)
            h_scales = work.tile([P, PASSES * P], U8, align_bytes=64)
            nc.vector.quantize_mx(out=h_codes[:].bitcast(FP8X4), scales=h_scales[:], in_=tiles["h_grp", b][:])
            tiles["h_codes", b] = h_codes
            tiles["h_scales", b] = h_scales

        def down(b):
            if not exists(b):
                return
            a_ps = psum_a.tile([P, PACK, P], F32)
            for t in range(PACK):
                for g in range(PASSES):
                    w_cols = slice((t * PASSES + g) * P, (t * PASSES + g + 1) * P)
                    x_cols = slice(g * P, (g + 1) * P)
                    nc.tensor.matmul_mx(
                        out=a_ps[:, t, :],
                        lhsT=wd_codes[:, w_cols].bitcast(FP8X4),
                        lhsT_scale=wd_scales[:, w_cols],
                        rhs=tiles["h_codes", b][:, x_cols].bitcast(FP8X4),
                        rhs_scale=tiles["h_scales", b][:, x_cols],
                        start=(g == 0),
                        stop=(g == PASSES - 1),
                    )
            tiles["a", b] = a_ps

        def silu(b):
            if not exists(b):
                return
            view_grp = work.tile([P, PACK * P], BF16, align_bytes=64)
            nc.scalar.activation(
                out=view_grp[:].rearrange("p (n t) -> p n t", t=PACK),
                in_=tiles["a", b][:].rearrange("p t n -> p n t"),
                func=ACT.Silu,
            )
            tiles["view_grp", b] = view_grp

        def quantise_view(b):
            if not exists(b):
                return
            cols = slice(b * P, (b + 1) * P)
            nc.vector.quantize_mx(
                out=view_codes[:, cols].bitcast(FP8X4), scales=view_scales[:, cols], in_=tiles["view_grp", b][:]
            )

        def up(b):
            if not exists(b):
                return
            cols = slice(b * P, (b + 1) * P)
            for c in range(D // BANK):
                d_cols = slice(c * BANK, (c + 1) * BANK)
                upd = psum_o.tile([P, BANK], F32, tag="wide")
                nc.tensor.matmul_mx(
                    out=upd[:],
                    lhsT=view_codes[:, cols].bitcast(FP8X4),
                    lhsT_scale=view_scales[:, cols],
                    rhs=wu_codes[:, d_cols].bitcast(FP8X4),
                    rhs_scale=wu_scales[:, d_cols],
                    start=True,
                    stop=True,
                )
                tiles["upd", b, c] = upd

        def finish(b):
            if not exists(b):
                return
            for c in range(D // BANK):
                d_cols = slice(c * BANK, (c + 1) * BANK)
                out_sb = results.tile([P, BANK], F32)
                nc.vector.scalar_tensor_tensor(
                    out=out_sb[:],
                    in0=tiles["upd", b, c][:],
                    scalar=gate_eighth[:, 0:1],
                    in1=h_all[:, b, d_cols],
                    op0=ALU.mult,
                    op1=ALU.add,
                )
                nc.sync.dma_start(out=out_rows[b * P : (b + 1) * P, d_cols], in_=out_sb[:])

        for n in range(-1, BLOCKS + 3):
            square_sum(n + 1)
            normalise(n)
            for t in (2 * n + 2, 2 * n + 3):
                group_w_down(t)
                quantise_w_down(t - 1)
            transpose_h(n)
            quantise_h(n - 1)
            down(n - 1)
            w_up_turn(2 * n - 2)
            group_h(n)
            if n == 2:
                gate_on_scalar()
            quantise_view(n - 2)
            finish(n - 3)
            w_up_turn(2 * n - 1)
            up(n - 2)
            silu(n - 1)
            if n == 2:
                gate_on_vector()
